import numpy as np
import ml_dtypes

BF16 = ml_dtypes.bfloat16


def bf(x):
    return np.asarray(x, np.float32).astype(BF16)


def f32(x):
    return np.asarray(x, np.float32)


def f64(x):
    return np.asarray(x).astype(np.float64)


def striped(idx):
    return np.tile(idx.reshape(-1, 16).T, (8, 1))


D, C, S, N = 128, 512, 1024, 256


def setup_inputs():
    return {
        "base": f32(-20.0 + 4.0 * np.random.standard_normal((C, S))),
        "samples": f32(0.5 * np.random.standard_normal((D, N))),
        "mask": f32(np.random.uniform(size=(D, N))),
        "cent": f32(0.5 * np.random.standard_normal((D, C))),
        "sd": f32(np.random.uniform(size=(D, 1)) + 0.5),
        "log_marginal": f32(np.random.standard_normal((C, 1))),
        "offs": striped(np.random.permutation(S)[:N]),
    }


def reference(base, samples, mask, cent, sd, log_marginal, offs):
    idx = offs[:16].T.reshape(-1)
    a = f64(samples)
    b = f64(cent)
    r = f64(mask) / f64(sd)
    q = r * r
    a_d = np.sum(q * a * a, axis=0, keepdims=True)
    b_d = (b * b).T @ q
    cross = b.T @ (q * a)
    dist = np.maximum(a_d - 2.0 * cross + b_d, 0.0)
    nh = -0.5 * dist
    lp = f64(log_marginal) - np.log(np.sum(np.exp(f64(log_marginal))))
    out = f64(base).copy()
    out[:, idx] = lp + nh
    return out

@@ -1,0 +1,84 @@
+import concourse.mybir as mybir
+
+F32, BF16, U16 = mybir.dt.float32, mybir.dt.bfloat16, mybir.dt.uint16
+ALU = mybir.AluOpType
+FUNC = mybir.ActivationFunctionType
+
+P = 128
+D, C, S, N = 128, 512, 1024, 256
+K = C // P
+
+FLOPS = 2 * D * C * N * 2 + 2 * D * N
+
+
+def tile_rmm_kernel(tc, base, samples, mask, cent, sd, log_marginal, offs, out):
+    nc = tc.nc
+    base_blocks = base.rearrange("(p k) s -> k p s", k=K)
+    out_blocks = out.rearrange("(p k) s -> k p s", k=K)
+
+    with (
+        tc.tile_pool(name="held", bufs=1) as held,
+        tc.psum_pool(name="psum", bufs=1) as psum,
+    ):
+        offsets = held.tile([P, N // 16], U16, name="offsets")
+        nc.sync.dma_start(offsets[:], offs)
+        prior_all = held.tile([P, C], F32, name="prior_all")
+        nc.sync.dma_start(prior_all[:], log_marginal.rearrange("c one -> (c one)").partition_broadcast(P))
+        prior_own = held.tile([P, K], F32, name="prior_own")
+        nc.scalar.dma_start(prior_own[:], log_marginal.rearrange("(p k) one -> p (k one)", k=K))
+        sd_sb = held.tile([P, 1], F32, name="sd_sb")
+        nc.scalar.dma_start(sd_sb[:], sd)
+        mask_sb = held.tile([P, N], F32, name="mask_sb")
+        nc.sync.dma_start(mask_sb[:], mask)
+        samples_sb = held.tile([P, N], F32, name="samples_sb")
+        nc.sync.dma_start(samples_sb[:], samples)
+        cent_sb = held.tile([P, C], F32, name="cent_sb")
+        nc.sync.dma_start(cent_sb[:], cent)
+        windows = [held.tile([P, S], F32, name=f"window{k}") for k in range(K)]
+        for k in range(K):
+            nc.sync.dma_start(windows[k][:], base_blocks[k])
+
+        neg_max = held.tile([P, 1], F32, name="neg_max")
+        nc.vector.tensor_reduce(neg_max[:], prior_all[:], mybir.AxisListType.X, ALU.max, negate=True)
+        exp_all = held.tile([P, C], F32, name="exp_all")
+        exp_sum = held.tile([P, 1], F32, name="exp_sum")
+        nc.scalar.activation(exp_all[:], prior_all[:], FUNC.Exp, bias=neg_max[:], accum_out=exp_sum[:])
+        log_sum = held.tile([P, 1], F32, name="log_sum")
+        nc.scalar.activation(log_sum[:], exp_sum[:], FUNC.Ln)
+        shifted = held.tile([P, K], F32, name="shifted")
+        nc.vector.tensor_scalar(shifted[:], prior_own[:], neg_max[:], None, ALU.add)
+        lp_wide = [held.tile([P, N], F32, name=f"lp_wide{k}") for k in range(K)]
+        for k in range(K):
+            nc.scalar.activation(
+                lp_wide[k][:], log_sum[:].to_broadcast([P, N]), FUNC.Identity, bias=shifted[:, k : k + 1], scale=-1.0
+            )
+
+        inv_var = held.tile([P, 1], F32, name="inv_var")
+        nc.vector.reciprocal(inv_var[:], sd_sb[:])
+        nc.vector.tensor_tensor(inv_var[:], inv_var[:], inv_var[:], ALU.mult)
+        masked = held.tile([P, N], F32, name="masked")
+        nc.gpsimd.tensor_tensor(masked[:], mask_sb[:], samples_sb[:], ALU.mult)
+        q_bf = held.tile([P, N], BF16, name="q_bf")
+        nc.vector.scalar_tensor_tensor(q_bf[:], mask_sb[:], inv_var[:], mask_sb[:], ALU.mult, ALU.mult)
+        qa_bf = held.tile([P, N], BF16, name="qa_bf")
+        nc.vector.scalar_tensor_tensor(qa_bf[:], masked[:], inv_var[:], mask_sb[:], ALU.mult, ALU.mult)
+        qaa_bf = held.tile([P, N], BF16, name="qaa_bf")
+        nc.vector.scalar_tensor_tensor(qaa_bf[:], masked[:], inv_var[:], masked[:], ALU.mult, ALU.mult)
+
+        cent_by_block = cent_sb[:].rearrange("d (p k) -> d k p", k=K)
+        cent_m2_bf = held.tile([P, K, P], BF16, name="cent_m2_bf")
+        nc.vector.tensor_scalar(cent_m2_bf[:], cent_by_block, -2.0, None, ALU.mult)
+        cent_sq_bf = held.tile([P, K, P], BF16, name="cent_sq_bf")
+        nc.gpsimd.tensor_tensor(cent_sq_bf[:], cent_by_block, cent_by_block, ALU.mult)
+        ones_bf = held.tile([P, P], BF16, name="ones_bf")
+        nc.gpsimd.memset(ones_bf[:], 1.0)
+
+        for k in range(K):
+            dist = psum.tile([P, N], F32, name=f"dist{k}")
+            nc.tensor.matmul(dist[:], ones_bf[:], qaa_bf[:], start=True, stop=False)
+            nc.tensor.matmul(dist[:], cent_m2_bf[:, k, :], qa_bf[:], start=False, stop=False)
+            nc.tensor.matmul(dist[:], cent_sq_bf[:, k, :], q_bf[:], start=False, stop=True)
+            nh = held.tile([P, N], F32, name=f"nh{k}")
+            nc.vector.tensor_scalar(nh[:], dist[:], 0.0, -0.5, ALU.max, ALU.mult)
+            nc.vector.tensor_tensor(windows[k][:].indirect(offsets[:]), nh[:], lp_wide[k][:], ALU.add)
+            nc.sync.dma_start(out_blocks[k], windows[k][:])

@@ -38,6 +38,9 @@ def tile_rmm_kernel(tc, base, samples, mask, cent, sd, log_marginal, offs, out):
         for k in range(K):
             nc.sync.dma_start(windows[k][:], base_blocks[k])
 
+        unit = held.tile([P, 1], F32, name="unit")
+        nc.vector.memset(unit[:], 0.0)
+        nc.scalar.activation(unit[:], unit[:], FUNC.Exp)
         neg_max = held.tile([P, 1], F32, name="neg_max")
         nc.vector.tensor_reduce(neg_max[:], prior_all[:], mybir.AxisListType.X, ALU.max, negate=True)
         exp_all = held.tile([P, C], F32, name="exp_all")

@@ -82,6 +82,11 @@ def tile_rmm_kernel(tc, base, samples, mask, cent, sd, log_marginal, offs, out):
             nc.tensor.matmul(dist[:], cent_m2_bf[:, k, :], qa_bf[:], start=False, stop=False)
             nc.tensor.matmul(dist[:], cent_sq_bf[:, k, :], q_bf[:], start=False, stop=True)
             nh = held.tile([P, N], F32, name=f"nh{k}")
-            nc.vector.tensor_scalar(nh[:], dist[:], 0.0, -0.5, ALU.max, ALU.mult)
+            if k == 0:
+                nc.vector.tensor_scalar(nh[:], dist[:], 0.0, -0.5, ALU.max, ALU.mult)
+            else:
+                half_dist = held.tile([P, N], F32, name=f"half_dist{k}")
+                nc.scalar.activation(half_dist[:], dist[:], FUNC.Relu, scale=0.5)
+                nc.scalar.mul(nh[:], half_dist[:], -1.0)
             nc.vector.tensor_tensor(windows[k][:].indirect(offsets[:]), nh[:], lp_wide[k][:], ALU.add)
             nc.sync.dma_start(out_blocks[k], windows[k][:])

@@ -24,10 +24,10 @@ def tile_rmm_kernel(tc, base, samples, mask, cent, sd, log_marginal, offs, out):
         nc.sync.dma_start(offsets[:], offs)
         prior_all = held.tile([P, C], F32, name="prior_all")
         nc.sync.dma_start(prior_all[:], log_marginal.rearrange("c one -> (c one)").partition_broadcast(P))
-        prior_own = held.tile([P, K], F32, name="prior_own")
-        nc.scalar.dma_start(prior_own[:], log_marginal.rearrange("(p k) one -> p (k one)", k=K))
         sd_sb = held.tile([P, 1], F32, name="sd_sb")
         nc.scalar.dma_start(sd_sb[:], sd)
+        prior_own = held.tile([P, K], F32, name="prior_own")
+        nc.scalar.dma_start(prior_own[:], log_marginal.rearrange("(p k) one -> p (k one)", k=K))
         mask_sb = held.tile([P, N], F32, name="mask_sb")
         nc.sync.dma_start(mask_sb[:], mask)
         samples_sb = held.tile([P, N], F32, name="samples_sb")
@@ -38,14 +38,30 @@ def tile_rmm_kernel(tc, base, samples, mask, cent, sd, log_marginal, offs, out):
         for k in range(K):
             nc.sync.dma_start(windows[k][:], base_blocks[k])
 
+        ones_bf = held.tile([P, P], BF16, name="ones_bf")
+        nc.gpsimd.memset(ones_bf[:], 1.0)
+        ones_f32 = held.tile([P, P], F32, name="ones_f32")
+        nc.gpsimd.memset(ones_f32[:], 1.0)
         unit = held.tile([P, 1], F32, name="unit")
-        nc.vector.memset(unit[:], 0.0)
+        nc.gpsimd.memset(unit[:], 0.0)
         nc.scalar.activation(unit[:], unit[:], FUNC.Exp)
+
+        inv_sd = held.tile([P, 1], F32, name="inv_sd")
+        nc.vector.reciprocal(inv_sd[:], sd_sb[:])
+        inv_var = held.tile([P, 1], F32, name="inv_var")
+        nc.vector.tensor_tensor(inv_var[:], inv_sd[:], inv_sd[:], ALU.mult)
+        inv_var_m2 = held.tile([P, 1], F32, name="inv_var_m2")
+        nc.vector.tensor_scalar(inv_var_m2[:], inv_var[:], -2.0, None, ALU.mult)
+        q_bf = held.tile([P, N], BF16, name="q_bf")
+        nc.scalar.activation(q_bf[:], mask_sb[:], FUNC.Square, scale=inv_sd[:])
+
         neg_max = held.tile([P, 1], F32, name="neg_max")
         nc.vector.tensor_reduce(neg_max[:], prior_all[:], mybir.AxisListType.X, ALU.max, negate=True)
-        exp_all = held.tile([P, C], F32, name="exp_all")
-        exp_sum = held.tile([P, 1], F32, name="exp_sum")
-        nc.scalar.activation(exp_all[:], prior_all[:], FUNC.Exp, bias=neg_max[:], accum_out=exp_sum[:])
+        exp_own = held.tile([P, K], F32, name="exp_own")
+        exp_own_sum = held.tile([P, 1], F32, name="exp_own_sum")
+        nc.scalar.activation(exp_own[:], prior_own[:], FUNC.Exp, bias=neg_max[:], accum_out=exp_own_sum[:])
+        exp_sum = psum.tile([P, 1], F32, name="exp_sum")
+        nc.tensor.matmul(exp_sum[:], ones_f32[:], exp_own_sum[:], start=True, stop=True)
         log_sum = held.tile([P, 1], F32, name="log_sum")
         nc.scalar.activation(log_sum[:], exp_sum[:], FUNC.Ln)
         shifted = held.tile([P, K], F32, name="shifted")
@@ -56,30 +72,25 @@ def tile_rmm_kernel(tc, base, samples, mask, cent, sd, log_marginal, offs, out):
                 lp_wide[k][:], log_sum[:].to_broadcast([P, N]), FUNC.Identity, bias=shifted[:, k : k + 1], scale=-1.0
             )
 
-        inv_var = held.tile([P, 1], F32, name="inv_var")
-        nc.vector.reciprocal(inv_var[:], sd_sb[:])
-        nc.vector.tensor_tensor(inv_var[:], inv_var[:], inv_var[:], ALU.mult)
         masked = held.tile([P, N], F32, name="masked")
-        nc.gpsimd.tensor_tensor(masked[:], mask_sb[:], samples_sb[:], ALU.mult)
-        q_bf = held.tile([P, N], BF16, name="q_bf")
-        nc.vector.scalar_tensor_tensor(q_bf[:], mask_sb[:], inv_var[:], mask_sb[:], ALU.mult, ALU.mult)
-        qa_bf = held.tile([P, N], BF16, name="qa_bf")
-        nc.vector.scalar_tensor_tensor(qa_bf[:], masked[:], inv_var[:], mask_sb[:], ALU.mult, ALU.mult)
+        nc.vector.tensor_tensor(masked[:], mask_sb[:], samples_sb[:], ALU.mult)
         qaa_bf = held.tile([P, N], BF16, name="qaa_bf")
         nc.vector.scalar_tensor_tensor(qaa_bf[:], masked[:], inv_var[:], masked[:], ALU.mult, ALU.mult)
+        qa_m2_bf = held.tile([P, N], BF16, name="qa_m2_bf")
+        nc.vector.scalar_tensor_tensor(qa_m2_bf[:], masked[:], inv_var_m2[:], mask_sb[:], ALU.mult, ALU.mult)
 
         cent_by_block = cent_sb[:].rearrange("d (p k) -> d k p", k=K)
-        cent_m2_bf = held.tile([P, K, P], BF16, name="cent_m2_bf")
-        nc.vector.tensor_scalar(cent_m2_bf[:], cent_by_block, -2.0, None, ALU.mult)
+        cent_bf = held.tile([P, K, P], BF16, name="cent_bf")
         cent_sq_bf = held.tile([P, K, P], BF16, name="cent_sq_bf")
-        nc.gpsimd.tensor_tensor(cent_sq_bf[:], cent_by_block, cent_by_block, ALU.mult)
-        ones_bf = held.tile([P, P], BF16, name="ones_bf")
-        nc.gpsimd.memset(ones_bf[:], 1.0)
+        for engine, blocks in ((nc.vector, slice(0, 1)), (nc.gpsimd, slice(1, K))):
+            cent_part = cent_by_block[:, blocks, :]
+            engine.tensor_copy(cent_bf[:, blocks, :], cent_part)
+            engine.tensor_tensor(cent_sq_bf[:, blocks, :], cent_part, cent_part, ALU.mult)
 
         for k in range(K):
             dist = psum.tile([P, N], F32, name=f"dist{k}")
             nc.tensor.matmul(dist[:], ones_bf[:], qaa_bf[:], start=True, stop=False)
-            nc.tensor.matmul(dist[:], cent_m2_bf[:, k, :], qa_bf[:], start=False, stop=False)
+            nc.tensor.matmul(dist[:], cent_bf[:, k, :], qa_m2_bf[:], start=False, stop=False)
             nc.tensor.matmul(dist[:], cent_sq_bf[:, k, :], q_bf[:], start=False, stop=True)
             nh = held.tile([P, N], F32, name=f"nh{k}")
             if k == 0:

@@ -64,34 +64,35 @@ def tile_rmm_kernel(tc, base, samples, mask, cent, sd, log_marginal, offs, out):
         nc.tensor.matmul(exp_sum[:], ones_f32[:], exp_own_sum[:], start=True, stop=True)
         log_sum = held.tile([P, 1], F32, name="log_sum")
         nc.scalar.activation(log_sum[:], exp_sum[:], FUNC.Ln)
-        shifted = held.tile([P, K], F32, name="shifted")
-        nc.vector.tensor_scalar(shifted[:], prior_own[:], neg_max[:], None, ALU.add)
-        lp_wide = [held.tile([P, N], F32, name=f"lp_wide{k}") for k in range(K)]
-        for k in range(K):
-            nc.scalar.activation(
-                lp_wide[k][:], log_sum[:].to_broadcast([P, N]), FUNC.Identity, bias=shifted[:, k : k + 1], scale=-1.0
-            )
 
         masked = held.tile([P, N], F32, name="masked")
         nc.vector.tensor_tensor(masked[:], mask_sb[:], samples_sb[:], ALU.mult)
+        shifted = held.tile([P, K], F32, name="shifted")
+        nc.vector.tensor_scalar(shifted[:], prior_own[:], neg_max[:], None, ALU.add)
         qaa_bf = held.tile([P, N], BF16, name="qaa_bf")
         nc.vector.scalar_tensor_tensor(qaa_bf[:], masked[:], inv_var[:], masked[:], ALU.mult, ALU.mult)
-        qa_m2_bf = held.tile([P, N], BF16, name="qa_m2_bf")
-        nc.vector.scalar_tensor_tensor(qa_m2_bf[:], masked[:], inv_var_m2[:], mask_sb[:], ALU.mult, ALU.mult)
 
         cent_by_block = cent_sb[:].rearrange("d (p k) -> d k p", k=K)
         cent_bf = held.tile([P, K, P], BF16, name="cent_bf")
         cent_sq_bf = held.tile([P, K, P], BF16, name="cent_sq_bf")
         for engine, blocks in ((nc.vector, slice(0, 1)), (nc.gpsimd, slice(1, K))):
             cent_part = cent_by_block[:, blocks, :]
-            engine.tensor_copy(cent_bf[:, blocks, :], cent_part)
             engine.tensor_tensor(cent_sq_bf[:, blocks, :], cent_part, cent_part, ALU.mult)
+            engine.tensor_copy(cent_bf[:, blocks, :], cent_part)
+        qa_m2_bf = held.tile([P, N], BF16, name="qa_m2_bf")
+        nc.vector.scalar_tensor_tensor(qa_m2_bf[:], masked[:], inv_var_m2[:], mask_sb[:], ALU.mult, ALU.mult)
+
+        lp_wide = [held.tile([P, N], F32, name=f"lp_wide{k}") for k in range(K)]
+        for k in range(K):
+            nc.scalar.activation(
+                lp_wide[k][:], log_sum[:].to_broadcast([P, N]), FUNC.Identity, bias=shifted[:, k : k + 1], scale=-1.0
+            )
 
         for k in range(K):
             dist = psum.tile([P, N], F32, name=f"dist{k}")
             nc.tensor.matmul(dist[:], ones_bf[:], qaa_bf[:], start=True, stop=False)
-            nc.tensor.matmul(dist[:], cent_bf[:, k, :], qa_m2_bf[:], start=False, stop=False)
-            nc.tensor.matmul(dist[:], cent_sq_bf[:, k, :], q_bf[:], start=False, stop=True)
+            nc.tensor.matmul(dist[:], cent_sq_bf[:, k, :], q_bf[:], start=False, stop=False)
+            nc.tensor.matmul(dist[:], cent_bf[:, k, :], qa_m2_bf[:], start=False, stop=True)
             nh = held.tile([P, N], F32, name=f"nh{k}")
             if k == 0:
                 nc.vector.tensor_scalar(nh[:], dist[:], 0.0, -0.5, ALU.max, ALU.mult)

@@ -60,6 +60,7 @@ def tile_rmm_kernel(tc, base, samples, mask, cent, sd, log_marginal, offs, out):
         exp_own = held.tile([P, K], F32, name="exp_own")
         exp_own_sum = held.tile([P, 1], F32, name="exp_own_sum")
         nc.scalar.activation(exp_own[:], prior_own[:], FUNC.Exp, bias=neg_max[:], accum_out=exp_own_sum[:])
+        nc.scalar.activation(unit[:], unit[:], FUNC.Ln)
         exp_sum = psum.tile([P, 1], F32, name="exp_sum")
         nc.tensor.matmul(exp_sum[:], ones_f32[:], exp_own_sum[:], start=True, stop=True)
         log_sum = held.tile([P, 1], F32, name="log_sum")

@@ -8,6 +8,9 @@ P = 128
 D, C, S, N = 128, 512, 1024, 256
 K = C // P
 
+WARM_COLUMNS = 512
+WARM_MATMULS = 8
+
 FLOPS = 2 * D * C * N * 2 + 2 * D * N
 
 
@@ -42,6 +45,11 @@ def tile_rmm_kernel(tc, base, samples, mask, cent, sd, log_marginal, offs, out):
         nc.gpsimd.memset(ones_bf[:], 1.0)
         ones_f32 = held.tile([P, P], F32, name="ones_f32")
         nc.gpsimd.memset(ones_f32[:], 1.0)
+        warm_rhs = held.tile([P, WARM_COLUMNS], BF16, name="warm_rhs")
+        nc.gpsimd.memset(warm_rhs[:], 1.0)
+        warm_sum = psum.tile([P, WARM_COLUMNS], F32, name="warm_sum")
+        for i in range(WARM_MATMULS):
+            nc.tensor.matmul(warm_sum[:], ones_bf[:], warm_rhs[:], start=(i == 0), stop=(i == WARM_MATMULS - 1))
         unit = held.tile([P, 1], F32, name="unit")
         nc.gpsimd.memset(unit[:], 0.0)
         nc.scalar.activation(unit[:], unit[:], FUNC.Exp)
@@ -60,40 +68,38 @@ def tile_rmm_kernel(tc, base, samples, mask, cent, sd, log_marginal, offs, out):
         exp_own = held.tile([P, K], F32, name="exp_own")
         exp_own_sum = held.tile([P, 1], F32, name="exp_own_sum")
         nc.scalar.activation(exp_own[:], prior_own[:], FUNC.Exp, bias=neg_max[:], accum_out=exp_own_sum[:])
-        nc.scalar.activation(unit[:], unit[:], FUNC.Ln)
         exp_sum = psum.tile([P, 1], F32, name="exp_sum")
         nc.tensor.matmul(exp_sum[:], ones_f32[:], exp_own_sum[:], start=True, stop=True)
         log_sum = held.tile([P, 1], F32, name="log_sum")
         nc.scalar.activation(log_sum[:], exp_sum[:], FUNC.Ln)
-
-        masked = held.tile([P, N], F32, name="masked")
-        nc.vector.tensor_tensor(masked[:], mask_sb[:], samples_sb[:], ALU.mult)
         shifted = held.tile([P, K], F32, name="shifted")
         nc.vector.tensor_scalar(shifted[:], prior_own[:], neg_max[:], None, ALU.add)
-        qaa_bf = held.tile([P, N], BF16, name="qaa_bf")
-        nc.vector.scalar_tensor_tensor(qaa_bf[:], masked[:], inv_var[:], masked[:], ALU.mult, ALU.mult)
-
-        cent_by_block = cent_sb[:].rearrange("d (p k) -> d k p", k=K)
-        cent_bf = held.tile([P, K, P], BF16, name="cent_bf")
-        cent_sq_bf = held.tile([P, K, P], BF16, name="cent_sq_bf")
-        for engine, blocks in ((nc.vector, slice(0, 1)), (nc.gpsimd, slice(1, K))):
-            cent_part = cent_by_block[:, blocks, :]
-            engine.tensor_tensor(cent_sq_bf[:, blocks, :], cent_part, cent_part, ALU.mult)
-            engine.tensor_copy(cent_bf[:, blocks, :], cent_part)
-        qa_m2_bf = held.tile([P, N], BF16, name="qa_m2_bf")
-        nc.vector.scalar_tensor_tensor(qa_m2_bf[:], masked[:], inv_var_m2[:], mask_sb[:], ALU.mult, ALU.mult)
-
         lp_wide = [held.tile([P, N], F32, name=f"lp_wide{k}") for k in range(K)]
         for k in range(K):
             nc.scalar.activation(
                 lp_wide[k][:], log_sum[:].to_broadcast([P, N]), FUNC.Identity, bias=shifted[:, k : k + 1], scale=-1.0
             )
 
+        masked = held.tile([P, N], F32, name="masked")
+        nc.vector.tensor_tensor(masked[:], mask_sb[:], samples_sb[:], ALU.mult)
+        qaa_bf = held.tile([P, N], BF16, name="qaa_bf")
+        nc.vector.scalar_tensor_tensor(qaa_bf[:], masked[:], inv_var[:], masked[:], ALU.mult, ALU.mult)
+        qa_m2_bf = held.tile([P, N], BF16, name="qa_m2_bf")
+        nc.vector.scalar_tensor_tensor(qa_m2_bf[:], masked[:], inv_var_m2[:], mask_sb[:], ALU.mult, ALU.mult)
+
+        cent_by_block = cent_sb[:].rearrange("d (p k) -> d k p", k=K)
+        cent_bf = held.tile([P, K, P], BF16, name="cent_bf")
+        cent_sq_bf = held.tile([P, K, P], BF16, name="cent_sq_bf")
+        for engine, blocks in ((nc.vector, slice(0, 1)), (nc.gpsimd, slice(1, K))):
+            cent_part = cent_by_block[:, blocks, :]
+            engine.tensor_copy(cent_bf[:, blocks, :], cent_part)
+            engine.tensor_tensor(cent_sq_bf[:, blocks, :], cent_part, cent_part, ALU.mult)
+
         for k in range(K):
             dist = psum.tile([P, N], F32, name=f"dist{k}")
             nc.tensor.matmul(dist[:], ones_bf[:], qaa_bf[:], start=True, stop=False)
-            nc.tensor.matmul(dist[:], cent_sq_bf[:, k, :], q_bf[:], start=False, stop=False)
-            nc.tensor.matmul(dist[:], cent_bf[:, k, :], qa_m2_bf[:], start=False, stop=True)
+            nc.tensor.matmul(dist[:], cent_bf[:, k, :], qa_m2_bf[:], start=False, stop=False)
+            nc.tensor.matmul(dist[:], cent_sq_bf[:, k, :], q_bf[:], start=False, stop=True)
             nh = held.tile([P, N], F32, name=f"nh{k}")
             if k == 0:
                 nc.vector.tensor_scalar(nh[:], dist[:], 0.0, -0.5, ALU.max, ALU.mult)

@@ -8,9 +8,6 @@ P = 128
 D, C, S, N = 128, 512, 1024, 256
 K = C // P
 
-WARM_COLUMNS = 512
-WARM_MATMULS = 8
-
 FLOPS = 2 * D * C * N * 2 + 2 * D * N
 
 
@@ -41,18 +38,14 @@ def tile_rmm_kernel(tc, base, samples, mask, cent, sd, log_marginal, offs, out):
         for k in range(K):
             nc.sync.dma_start(windows[k][:], base_blocks[k])
 
-        ones_bf = held.tile([P, P], BF16, name="ones_bf")
-        nc.gpsimd.memset(ones_bf[:], 1.0)
-        ones_f32 = held.tile([P, P], F32, name="ones_f32")
-        nc.gpsimd.memset(ones_f32[:], 1.0)
-        warm_rhs = held.tile([P, WARM_COLUMNS], BF16, name="warm_rhs")
-        nc.gpsimd.memset(warm_rhs[:], 1.0)
-        warm_sum = psum.tile([P, WARM_COLUMNS], F32, name="warm_sum")
-        for i in range(WARM_MATMULS):
-            nc.tensor.matmul(warm_sum[:], ones_bf[:], warm_rhs[:], start=(i == 0), stop=(i == WARM_MATMULS - 1))
         unit = held.tile([P, 1], F32, name="unit")
-        nc.gpsimd.memset(unit[:], 0.0)
+        nc.vector.memset(unit[:], 0.0)
         nc.scalar.activation(unit[:], unit[:], FUNC.Exp)
+
+        ones_bf = held.tile([P, P], BF16, name="ones_bf")
+        nc.vector.memset(ones_bf[:], 1.0)
+        ones_f32 = held.tile([P, P], F32, name="ones_f32")
+        nc.vector.memset(ones_f32[:], 1.0)
 
         inv_sd = held.tile([P, 1], F32, name="inv_sd")
         nc.vector.reciprocal(inv_sd[:], sd_sb[:])
@@ -68,17 +61,13 @@ def tile_rmm_kernel(tc, base, samples, mask, cent, sd, log_marginal, offs, out):
         exp_own = held.tile([P, K], F32, name="exp_own")
         exp_own_sum = held.tile([P, 1], F32, name="exp_own_sum")
         nc.scalar.activation(exp_own[:], prior_own[:], FUNC.Exp, bias=neg_max[:], accum_out=exp_own_sum[:])
+        nc.scalar.activation(unit[:], neg_max[:], FUNC.Ln, bias=1.0, scale=0.0)
         exp_sum = psum.tile([P, 1], F32, name="exp_sum")
         nc.tensor.matmul(exp_sum[:], ones_f32[:], exp_own_sum[:], start=True, stop=True)
         log_sum = held.tile([P, 1], F32, name="log_sum")
         nc.scalar.activation(log_sum[:], exp_sum[:], FUNC.Ln)
         shifted = held.tile([P, K], F32, name="shifted")
         nc.vector.tensor_scalar(shifted[:], prior_own[:], neg_max[:], None, ALU.add)
-        lp_wide = [held.tile([P, N], F32, name=f"lp_wide{k}") for k in range(K)]
-        for k in range(K):
-            nc.scalar.activation(
-                lp_wide[k][:], log_sum[:].to_broadcast([P, N]), FUNC.Identity, bias=shifted[:, k : k + 1], scale=-1.0
-            )
 
         masked = held.tile([P, N], F32, name="masked")
         nc.vector.tensor_tensor(masked[:], mask_sb[:], samples_sb[:], ALU.mult)
@@ -90,10 +79,10 @@ def tile_rmm_kernel(tc, base, samples, mask, cent, sd, log_marginal, offs, out):
         cent_by_block = cent_sb[:].rearrange("d (p k) -> d k p", k=K)
         cent_bf = held.tile([P, K, P], BF16, name="cent_bf")
         cent_sq_bf = held.tile([P, K, P], BF16, name="cent_sq_bf")
-        for engine, blocks in ((nc.vector, slice(0, 1)), (nc.gpsimd, slice(1, K))):
+        for blocks in (slice(0, 1), slice(1, K)):
             cent_part = cent_by_block[:, blocks, :]
-            engine.tensor_copy(cent_bf[:, blocks, :], cent_part)
-            engine.tensor_tensor(cent_sq_bf[:, blocks, :], cent_part, cent_part, ALU.mult)
+            nc.vector.tensor_copy(cent_bf[:, blocks, :], cent_part)
+            nc.vector.tensor_tensor(cent_sq_bf[:, blocks, :], cent_part, cent_part, ALU.mult)
 
         for k in range(K):
             dist = psum.tile([P, N], F32, name=f"dist{k}")
@@ -107,5 +96,9 @@ def tile_rmm_kernel(tc, base, samples, mask, cent, sd, log_marginal, offs, out):
                 half_dist = held.tile([P, N], F32, name=f"half_dist{k}")
                 nc.scalar.activation(half_dist[:], dist[:], FUNC.Relu, scale=0.5)
                 nc.scalar.mul(nh[:], half_dist[:], -1.0)
-            nc.vector.tensor_tensor(windows[k][:].indirect(offsets[:]), nh[:], lp_wide[k][:], ALU.add)
+            lp_wide = held.tile([P, N], F32, name=f"lp_wide{k}")
+            nc.scalar.activation(
+                lp_wide[:], log_sum[:].to_broadcast([P, N]), FUNC.Identity, bias=shifted[:, k : k + 1], scale=-1.0
+            )
+            nc.vector.tensor_tensor(windows[k][:].indirect(offsets[:]), nh[:], lp_wide[:], ALU.add)
             nc.sync.dma_start(out_blocks[k], windows[k][:])

@@ -13,8 +13,8 @@ FLOPS = 2 * D * C * N * 2 + 2 * D * N
 
 def tile_rmm_kernel(tc, base, samples, mask, cent, sd, log_marginal, offs, out):
     nc = tc.nc
-    base_blocks = base.rearrange("(p k) s -> k p s", k=K)
-    out_blocks = out.rearrange("(p k) s -> k p s", k=K)
+    base_blocks = base.rearrange("(k p) s -> k p s", p=P)
+    out_blocks = out.rearrange("(k p) s -> k p s", p=P)
 
     with (
         tc.tile_pool(name="held", bufs=1) as held,
@@ -27,7 +27,7 @@ def tile_rmm_kernel(tc, base, samples, mask, cent, sd, log_marginal, offs, out):
         sd_sb = held.tile([P, 1], F32, name="sd_sb")
         nc.scalar.dma_start(sd_sb[:], sd)
         prior_own = held.tile([P, K], F32, name="prior_own")
-        nc.scalar.dma_start(prior_own[:], log_marginal.rearrange("(p k) one -> p (k one)", k=K))
+        nc.scalar.dma_start(prior_own[:], log_marginal.rearrange("(k p) one -> p (k one)", p=P))
         mask_sb = held.tile([P, N], F32, name="mask_sb")
         nc.sync.dma_start(mask_sb[:], mask)
         samples_sb = held.tile([P, N], F32, name="samples_sb")
@@ -76,7 +76,7 @@ def tile_rmm_kernel(tc, base, samples, mask, cent, sd, log_marginal, offs, out):
         qa_m2_bf = held.tile([P, N], BF16, name="qa_m2_bf")
         nc.vector.scalar_tensor_tensor(qa_m2_bf[:], masked[:], inv_var_m2[:], mask_sb[:], ALU.mult, ALU.mult)
 
-        cent_by_block = cent_sb[:].rearrange("d (p k) -> d k p", k=K)
+        cent_by_block = cent_sb[:].rearrange("d (k p) -> d k p", p=P)
         cent_bf = held.tile([P, K, P], BF16, name="cent_bf")
         cent_sq_bf = held.tile([P, K, P], BF16, name="cent_sq_bf")
         for blocks in (slice(0, 1), slice(1, K)):

@@ -22,8 +22,8 @@ def tile_rmm_kernel(tc, base, samples, mask, cent, sd, log_marginal, offs, out):
     ):
         offsets = held.tile([P, N // 16], U16, name="offsets")
         nc.sync.dma_start(offsets[:], offs)
-        prior_all = held.tile([P, C], F32, name="prior_all")
-        nc.sync.dma_start(prior_all[:], log_marginal.rearrange("c one -> (c one)").partition_broadcast(P))
+        prior_row = held.tile([1, C], F32, name="prior_row")
+        nc.sync.dma_start(prior_row[:], log_marginal.rearrange("c one -> one c"))
         sd_sb = held.tile([P, 1], F32, name="sd_sb")
         nc.scalar.dma_start(sd_sb[:], sd)
         prior_own = held.tile([P, K], F32, name="prior_own")
@@ -56,8 +56,12 @@ def tile_rmm_kernel(tc, base, samples, mask, cent, sd, log_marginal, offs, out):
         q_bf = held.tile([P, N], BF16, name="q_bf")
         nc.scalar.activation(q_bf[:], mask_sb[:], FUNC.Square, scale=inv_sd[:])
 
+        neg_max_one = held.tile([1, 1], F32, name="neg_max_one")
+        nc.vector.tensor_reduce(neg_max_one[:], prior_row[:], mybir.AxisListType.X, ALU.max, negate=True)
+        neg_max_psum = psum.tile([P, 1], F32, name="neg_max_psum")
+        nc.tensor.matmul(neg_max_psum[:], ones_f32[0:1, :], neg_max_one[:], start=True, stop=True)
         neg_max = held.tile([P, 1], F32, name="neg_max")
-        nc.vector.tensor_reduce(neg_max[:], prior_all[:], mybir.AxisListType.X, ALU.max, negate=True)
+        nc.scalar.copy(neg_max[:], neg_max_psum[:])
         exp_own = held.tile([P, K], F32, name="exp_own")
         exp_own_sum = held.tile([P, 1], F32, name="exp_own_sum")
         nc.scalar.activation(exp_own[:], prior_own[:], FUNC.Exp, bias=neg_max[:], accum_out=exp_own_sum[:])

@@ -20,20 +20,22 @@ def tile_rmm_kernel(tc, base, samples, mask, cent, sd, log_marginal, offs, out):
         tc.tile_pool(name="held", bufs=1) as held,
         tc.psum_pool(name="psum", bufs=1) as psum,
     ):
+        prior_rows = held.tile([K, C], F32, name="prior_rows")
+        nc.sync.dma_start(prior_rows[:], log_marginal.rearrange("c one -> (c one)").partition_broadcast(K))
+        prior_part = held.tile([K, P], F32, name="prior_part")
+        nc.sync.dma_start(prior_part[:], log_marginal.rearrange("(k p) one -> k (p one)", p=P))
+        sd_sb = held.tile([P, 1], F32, name="sd_sb")
+        nc.sync.dma_start(sd_sb[:], sd)
         offsets = held.tile([P, N // 16], U16, name="offsets")
         nc.sync.dma_start(offsets[:], offs)
-        prior_row = held.tile([1, C], F32, name="prior_row")
-        nc.sync.dma_start(prior_row[:], log_marginal.rearrange("c one -> one c"))
-        sd_sb = held.tile([P, 1], F32, name="sd_sb")
-        nc.scalar.dma_start(sd_sb[:], sd)
-        prior_own = held.tile([P, K], F32, name="prior_own")
-        nc.scalar.dma_start(prior_own[:], log_marginal.rearrange("(k p) one -> p (k one)", p=P))
         mask_sb = held.tile([P, N], F32, name="mask_sb")
         nc.sync.dma_start(mask_sb[:], mask)
         samples_sb = held.tile([P, N], F32, name="samples_sb")
         nc.sync.dma_start(samples_sb[:], samples)
         cent_sb = held.tile([P, C], F32, name="cent_sb")
         nc.sync.dma_start(cent_sb[:], cent)
+        prior_own = held.tile([P, K], F32, name="prior_own")
+        nc.sync.dma_start(prior_own[:], log_marginal.rearrange("(k p) one -> p (k one)", p=P))
         windows = [held.tile([P, S], F32, name=f"window{k}") for k in range(K)]
         for k in range(K):
             nc.sync.dma_start(windows[k][:], base_blocks[k])
@@ -49,30 +51,28 @@ def tile_rmm_kernel(tc, base, samples, mask, cent, sd, log_marginal, offs, out):
 
         inv_sd = held.tile([P, 1], F32, name="inv_sd")
         nc.vector.reciprocal(inv_sd[:], sd_sb[:])
+        q_bf = held.tile([P, N], BF16, name="q_bf")
+        nc.scalar.activation(q_bf[:], mask_sb[:], FUNC.Square, scale=inv_sd[:])
+
+        neg_max_k = held.tile([K, 1], F32, name="neg_max_k")
+        nc.vector.tensor_reduce(neg_max_k[:], prior_rows[:], mybir.AxisListType.X, ALU.max, negate=True)
+        exp_part = held.tile([K, P], F32, name="exp_part")
+        exp_part_sum = held.tile([K, 1], F32, name="exp_part_sum")
+        nc.scalar.activation(exp_part[:], prior_part[:], FUNC.Exp, bias=neg_max_k[:], accum_out=exp_part_sum[:])
+        nc.scalar.activation(unit[0:K, :], neg_max_k[:], FUNC.Ln, bias=1.0, scale=0.0)
+        exp_sum = psum.tile([P, 1], F32, name="exp_sum")
+        nc.tensor.matmul(exp_sum[:], ones_f32[0:K, :], exp_part_sum[:], start=True, stop=True)
+        log_sum = held.tile([P, 1], F32, name="log_sum")
+        nc.scalar.activation(log_sum[:], exp_sum[:], FUNC.Ln)
+        neg_max = psum.tile([P, 1], F32, name="neg_max")
+        nc.tensor.matmul(neg_max[:], ones_f32[0:1, :], neg_max_k[0:1, :], start=True, stop=True)
+        log_z = held.tile([P, 1], F32, name="log_z")
+        nc.scalar.activation(log_z[:], neg_max[:], FUNC.Identity, bias=log_sum[:], scale=-1.0)
+
         inv_var = held.tile([P, 1], F32, name="inv_var")
         nc.vector.tensor_tensor(inv_var[:], inv_sd[:], inv_sd[:], ALU.mult)
         inv_var_m2 = held.tile([P, 1], F32, name="inv_var_m2")
         nc.vector.tensor_scalar(inv_var_m2[:], inv_var[:], -2.0, None, ALU.mult)
-        q_bf = held.tile([P, N], BF16, name="q_bf")
-        nc.scalar.activation(q_bf[:], mask_sb[:], FUNC.Square, scale=inv_sd[:])
-
-        neg_max_one = held.tile([1, 1], F32, name="neg_max_one")
-        nc.vector.tensor_reduce(neg_max_one[:], prior_row[:], mybir.AxisListType.X, ALU.max, negate=True)
-        neg_max_psum = psum.tile([P, 1], F32, name="neg_max_psum")
-        nc.tensor.matmul(neg_max_psum[:], ones_f32[0:1, :], neg_max_one[:], start=True, stop=True)
-        neg_max = held.tile([P, 1], F32, name="neg_max")
-        nc.scalar.copy(neg_max[:], neg_max_psum[:])
-        exp_own = held.tile([P, K], F32, name="exp_own")
-        exp_own_sum = held.tile([P, 1], F32, name="exp_own_sum")
-        nc.scalar.activation(exp_own[:], prior_own[:], FUNC.Exp, bias=neg_max[:], accum_out=exp_own_sum[:])
-        nc.scalar.activation(unit[:], neg_max[:], FUNC.Ln, bias=1.0, scale=0.0)
-        exp_sum = psum.tile([P, 1], F32, name="exp_sum")
-        nc.tensor.matmul(exp_sum[:], ones_f32[:], exp_own_sum[:], start=True, stop=True)
-        log_sum = held.tile([P, 1], F32, name="log_sum")
-        nc.scalar.activation(log_sum[:], exp_sum[:], FUNC.Ln)
-        shifted = held.tile([P, K], F32, name="shifted")
-        nc.vector.tensor_scalar(shifted[:], prior_own[:], neg_max[:], None, ALU.add)
-
         masked = held.tile([P, N], F32, name="masked")
         nc.vector.tensor_tensor(masked[:], mask_sb[:], samples_sb[:], ALU.mult)
         qaa_bf = held.tile([P, N], BF16, name="qaa_bf")
@@ -102,7 +102,7 @@ def tile_rmm_kernel(tc, base, samples, mask, cent, sd, log_marginal, offs, out):
                 nc.scalar.mul(nh[:], half_dist[:], -1.0)
             lp_wide = held.tile([P, N], F32, name=f"lp_wide{k}")
             nc.scalar.activation(
-                lp_wide[:], log_sum[:].to_broadcast([P, N]), FUNC.Identity, bias=shifted[:, k : k + 1], scale=-1.0
+                lp_wide[:], log_z[:].to_broadcast([P, N]), FUNC.Identity, bias=prior_own[:, k : k + 1], scale=-1.0
             )
             nc.vector.tensor_tensor(windows[k][:].indirect(offsets[:]), nh[:], lp_wide[:], ALU.add)
             nc.sync.dma_start(out_blocks[k], windows[k][:])

@@ -51,15 +51,18 @@ def tile_rmm_kernel(tc, base, samples, mask, cent, sd, log_marginal, offs, out):
 
         inv_sd = held.tile([P, 1], F32, name="inv_sd")
         nc.vector.reciprocal(inv_sd[:], sd_sb[:])
+        inv_var = held.tile([P, 1], F32, name="inv_var")
+        nc.vector.tensor_tensor(inv_var[:], inv_sd[:], inv_sd[:], ALU.mult)
+        inv_var_m2 = held.tile([P, 1], F32, name="inv_var_m2")
+        nc.vector.tensor_scalar(inv_var_m2[:], inv_var[:], -2.0, None, ALU.mult)
         q_bf = held.tile([P, N], BF16, name="q_bf")
-        nc.scalar.activation(q_bf[:], mask_sb[:], FUNC.Square, scale=inv_sd[:])
+        nc.vector.scalar_tensor_tensor(q_bf[:], mask_sb[:], inv_var[:], mask_sb[:], ALU.mult, ALU.mult)
 
         neg_max_k = held.tile([K, 1], F32, name="neg_max_k")
         nc.vector.tensor_reduce(neg_max_k[:], prior_rows[:], mybir.AxisListType.X, ALU.max, negate=True)
         exp_part = held.tile([K, P], F32, name="exp_part")
         exp_part_sum = held.tile([K, 1], F32, name="exp_part_sum")
         nc.scalar.activation(exp_part[:], prior_part[:], FUNC.Exp, bias=neg_max_k[:], accum_out=exp_part_sum[:])
-        nc.scalar.activation(unit[0:K, :], neg_max_k[:], FUNC.Ln, bias=1.0, scale=0.0)
         exp_sum = psum.tile([P, 1], F32, name="exp_sum")
         nc.tensor.matmul(exp_sum[:], ones_f32[0:K, :], exp_part_sum[:], start=True, stop=True)
         log_sum = held.tile([P, 1], F32, name="log_sum")
@@ -69,10 +72,6 @@ def tile_rmm_kernel(tc, base, samples, mask, cent, sd, log_marginal, offs, out):
         log_z = held.tile([P, 1], F32, name="log_z")
         nc.scalar.activation(log_z[:], neg_max[:], FUNC.Identity, bias=log_sum[:], scale=-1.0)
 
-        inv_var = held.tile([P, 1], F32, name="inv_var")
-        nc.vector.tensor_tensor(inv_var[:], inv_sd[:], inv_sd[:], ALU.mult)
-        inv_var_m2 = held.tile([P, 1], F32, name="inv_var_m2")
-        nc.vector.tensor_scalar(inv_var_m2[:], inv_var[:], -2.0, None, ALU.mult)
         masked = held.tile([P, N], F32, name="masked")
         nc.vector.tensor_tensor(masked[:], mask_sb[:], samples_sb[:], ALU.mult)
         qaa_bf = held.tile([P, N], BF16, name="qaa_bf")

import concourse.mybir as mybir

F32, BF16, U16 = mybir.dt.float32, mybir.dt.bfloat16, mybir.dt.uint16
ALU = mybir.AluOpType
FUNC = mybir.ActivationFunctionType

P = 128
D, C, S, N = 128, 512, 1024, 256
K = C // P

FLOPS = 2 * D * C * N * 2 + 2 * D * N


def tile_rmm_kernel(tc, base, samples, mask, cent, sd, log_marginal, offs, out):
    nc = tc.nc
    base_blocks = base.rearrange("(k p) s -> k p s", p=P)
    out_blocks = out.rearrange("(k p) s -> k p s", p=P)

    with (
        tc.tile_pool(name="held", bufs=1) as held,
        tc.psum_pool(name="psum", bufs=1) as psum,
    ):
        prior_rows = held.tile([K, C], F32, name="prior_rows")
        nc.sync.dma_start(prior_rows[:], log_marginal.rearrange("c one -> (c one)").partition_broadcast(K))
        prior_part = held.tile([K, P], F32, name="prior_part")
        nc.sync.dma_start(prior_part[:], log_marginal.rearrange("(k p) one -> k (p one)", p=P))
        sd_sb = held.tile([P, 1], F32, name="sd_sb")
        nc.sync.dma_start(sd_sb[:], sd)
        offsets = held.tile([P, N // 16], U16, name="offsets")
        nc.sync.dma_start(offsets[:], offs)
        mask_sb = held.tile([P, N], F32, name="mask_sb")
        nc.sync.dma_start(mask_sb[:], mask)
        samples_sb = held.tile([P, N], F32, name="samples_sb")
        nc.sync.dma_start(samples_sb[:], samples)
        cent_sb = held.tile([P, C], F32, name="cent_sb")
        nc.sync.dma_start(cent_sb[:], cent)
        prior_own = held.tile([P, K], F32, name="prior_own")
        nc.sync.dma_start(prior_own[:], log_marginal.rearrange("(k p) one -> p (k one)", p=P))
        windows = [held.tile([P, S], F32, name=f"window{k}") for k in range(K)]
        for k in range(K):
            nc.sync.dma_start(windows[k][:], base_blocks[k])

        unit = held.tile([P, 1], F32, name="unit")
        nc.vector.memset(unit[:], 0.0)
        nc.scalar.activation(unit[:], unit[:], FUNC.Exp)

        ones_bf = held.tile([P, P], BF16, name="ones_bf")
        nc.vector.memset(ones_bf[:], 1.0)
        ones_f32 = held.tile([P, P], F32, name="ones_f32")
        nc.vector.memset(ones_f32[:], 1.0)

        inv_sd = held.tile([P, 1], F32, name="inv_sd")
        nc.vector.reciprocal(inv_sd[:], sd_sb[:])
        inv_var = held.tile([P, 1], F32, name="inv_var")
        nc.vector.tensor_tensor(inv_var[:], inv_sd[:], inv_sd[:], ALU.mult)
        inv_var_m2 = held.tile([P, 1], F32, name="inv_var_m2")
        nc.vector.tensor_scalar(inv_var_m2[:], inv_var[:], -2.0, None, ALU.mult)
        q_bf = held.tile([P, N], BF16, name="q_bf")
        nc.vector.scalar_tensor_tensor(q_bf[:], mask_sb[:], inv_var[:], mask_sb[:], ALU.mult, ALU.mult)

        neg_max_k = held.tile([K, 1], F32, name="neg_max_k")
        nc.vector.tensor_reduce(neg_max_k[:], prior_rows[:], mybir.AxisListType.X, ALU.max, negate=True)
        exp_part = held.tile([K, P], F32, name="exp_part")
        exp_part_sum = held.tile([K, 1], F32, name="exp_part_sum")
        nc.scalar.activation(exp_part[:], prior_part[:], FUNC.Exp, bias=neg_max_k[:], accum_out=exp_part_sum[:])
        exp_sum = psum.tile([P, 1], F32, name="exp_sum")
        nc.tensor.matmul(exp_sum[:], ones_f32[0:K, :], exp_part_sum[:], start=True, stop=True)
        log_sum = held.tile([P, 1], F32, name="log_sum")
        nc.scalar.activation(log_sum[:], exp_sum[:], FUNC.Ln)
        neg_max = psum.tile([P, 1], F32, name="neg_max")
        nc.tensor.matmul(neg_max[:], ones_f32[0:1, :], neg_max_k[0:1, :], start=True, stop=True)
        log_z = held.tile([P, 1], F32, name="log_z")
        nc.scalar.activation(log_z[:], neg_max[:], FUNC.Identity, bias=log_sum[:], scale=-1.0)

        masked = held.tile([P, N], F32, name="masked")
        nc.vector.tensor_tensor(masked[:], mask_sb[:], samples_sb[:], ALU.mult)
        qaa_bf = held.tile([P, N], BF16, name="qaa_bf")
        nc.vector.scalar_tensor_tensor(qaa_bf[:], masked[:], inv_var[:], masked[:], ALU.mult, ALU.mult)
        qa_m2_bf = held.tile([P, N], BF16, name="qa_m2_bf")
        nc.vector.scalar_tensor_tensor(qa_m2_bf[:], masked[:], inv_var_m2[:], mask_sb[:], ALU.mult, ALU.mult)

        cent_by_block = cent_sb[:].rearrange("d (k p) -> d k p", p=P)
        cent_bf = held.tile([P, K, P], BF16, name="cent_bf")
        cent_sq_bf = held.tile([P, K, P], BF16, name="cent_sq_bf")
        for blocks in (slice(0, 1), slice(1, K)):
            cent_part = cent_by_block[:, blocks, :]
            nc.vector.tensor_copy(cent_bf[:, blocks, :], cent_part)
            nc.vector.tensor_tensor(cent_sq_bf[:, blocks, :], cent_part, cent_part, ALU.mult)

        for k in range(K):
            dist = psum.tile([P, N], F32, name=f"dist{k}")
            nc.tensor.matmul(dist[:], ones_bf[:], qaa_bf[:], start=True, stop=False)
            nc.tensor.matmul(dist[:], cent_bf[:, k, :], qa_m2_bf[:], start=False, stop=False)
            nc.tensor.matmul(dist[:], cent_sq_bf[:, k, :], q_bf[:], start=False, stop=True)
            nh = held.tile([P, N], F32, name=f"nh{k}")
            if k == 0:
                nc.vector.tensor_scalar(nh[:], dist[:], 0.0, -0.5, ALU.max, ALU.mult)
            else:
                half_dist = held.tile([P, N], F32, name=f"half_dist{k}")
                nc.scalar.activation(half_dist[:], dist[:], FUNC.Relu, scale=0.5)
                nc.scalar.mul(nh[:], half_dist[:], -1.0)
            lp_wide = held.tile([P, N], F32, name=f"lp_wide{k}")
            nc.scalar.activation(
                lp_wide[:], log_z[:].to_broadcast([P, N]), FUNC.Identity, bias=prior_own[:, k : k + 1], scale=-1.0
            )
            nc.vector.tensor_tensor(windows[k][:].indirect(offsets[:]), nh[:], lp_wide[:], ALU.add)
            nc.sync.dma_start(out_blocks[k], windows[k][:])
